import numpy as np
import ml_dtypes

BF16 = ml_dtypes.bfloat16


def bf(x):
    return np.asarray(x, np.float32).astype(BF16)


def f32(x):
    return np.asarray(x, np.float32)


def f64(x):
    return np.asarray(x).astype(np.float64)


def striped(idx):
    return np.tile(idx.reshape(-1, 16).T, (8, 1))


C, S, N, T, K, D, M = 128, 2048, 1024, 512, 2, 512, 1024
PE_BASE = 10000.0


def pos_code():
    arg = f32(np.arange(0, D, 2)) * np.float32(-np.log(PE_BASE) / D)
    ang = f64(f32(np.arange(T))[:, None] * f32(np.exp(f64(arg)))[None, :])
    pe = np.zeros((T, D))
    pe[:, 0::2] = np.sin(ang)
    pe[:, 1::2] = np.cos(ang)
    tail = pe[:, D - K * C:].T
    return np.concatenate([tail[r * C:(r + 1) * C] for r in range(K)], axis=1)


def setup_inputs():
    return {"emb": f32(np.random.standard_normal((C, S))), "pos": f32(pos_code()), "w": bf(np.random.standard_normal((K * C, M)) / np.sqrt(K * C)), "b": f32(0.1 * np.random.standard_normal((M, 1))), "offs": striped(np.random.permutation(np.tile(np.arange(S), 2))[:N])}


def reference(emb, pos, w, b, offs):
    idx = offs[:16].T.reshape(-1)
    xp = f64(emb)[:, idx] + f64(pos)
    xs = np.concatenate([xp[:, r * T:(r + 1) * T] for r in range(K)], axis=0)
    return f64(w).T @ xs + f64(b)

@@ -1,0 +1,62 @@
+import concourse.mybir as mybir
+
+F32 = mybir.dt.float32
+BF16 = mybir.dt.bfloat16
+U16 = mybir.dt.uint16
+ADD = mybir.AluOpType.add
+IDENTITY = mybir.ActivationFunctionType.Identity
+
+P = 128
+PLAYERS = 2048
+BALLS = 512
+ROLES = 2
+FEATURES = 1024
+BLOCKS = FEATURES // P
+PIECE = 256
+GROUP = 4
+
+FLOPS = 2 * ROLES * P * FEATURES * BALLS
+
+
+def tile_temporaltransformer_kernel(tc, emb, pos, w, b, offs, out):
+    nc = tc.nc
+
+    bias_rows = b.rearrange("(p j) one -> p (j one)", j=BLOCKS)
+    out_rows = out.rearrange("(p j) t -> p j t", j=BLOCKS)
+
+    with tc.tile_pool(name="held", bufs=1) as held, tc.psum_pool(name="psum", bufs=1) as psum:
+        offsets = held.tile([P, ROLES * BALLS // 16], U16, name="offsets")
+        nc.sync.dma_start(offsets[:], offs)
+        bias = held.tile([P, BLOCKS], F32, name="bias")
+        nc.sync.dma_start(bias[:], bias_rows)
+        table = held.tile([P, PLAYERS], F32, name="table")
+        nc.sync.dma_start(table[:], emb)
+        code = [held.tile([P, BALLS], F32, name=f"code{r}") for r in range(ROLES)]
+        for r in range(ROLES):
+            nc.sync.dma_start(code[r][:], pos[:, r * BALLS : (r + 1) * BALLS])
+        weights = [held.tile([P, FEATURES], BF16, name=f"weights{r}") for r in range(ROLES)]
+        for r in range(ROLES):
+            nc.sync.dma_start(weights[r][:], w[r * P : (r + 1) * P, :])
+
+        summed = [held.tile([P, BALLS], F32, name=f"summed{r}") for r in range(ROLES)]
+        rounded = [held.tile([P, BALLS], BF16, name=f"rounded{r}") for r in range(ROLES)]
+        for r in range(ROLES):
+            for t0 in range(0, BALLS, PIECE):
+                first = (r * BALLS + t0) // 16
+                picked = table[:].indirect(offsets[:, first : first + PIECE // 16])
+                nc.vector.tensor_tensor(summed[r][:, t0 : t0 + PIECE], picked, code[r][:, t0 : t0 + PIECE], ADD)
+                nc.scalar.copy(rounded[r][:, t0 : t0 + PIECE], summed[r][:, t0 : t0 + PIECE])
+
+        by_block = [weights[r][:].rearrange("c (p j) -> c j p", j=BLOCKS) for r in range(ROLES)]
+        banks = [psum.tile([P, BALLS], F32, name=f"bank{j}") for j in range(BLOCKS)]
+        result = held.tile([P, BLOCKS, BALLS], F32, name="result")
+        for j0 in range(0, BLOCKS, GROUP):
+            for j in range(j0, j0 + GROUP):
+                nc.tensor.matmul(banks[j][:], by_block[0][:, j, :], rounded[0][:], start=True, stop=False)
+            for j in range(j0, j0 + GROUP):
+                nc.tensor.matmul(banks[j][:], by_block[1][:, j, :], rounded[1][:], start=False, stop=True)
+                if j % 2 == 0:
+                    nc.scalar.activation(result[:, j, :], banks[j][:], IDENTITY, bias=bias[:, j : j + 1])
+                else:
+                    nc.vector.tensor_scalar_add(result[:, j, :], banks[j][:], bias[:, j : j + 1])
+                nc.sync.dma_start(out_rows[:, j, :], result[:, j, :])

@@ -12,8 +12,7 @@ BALLS = 512
 ROLES = 2
 FEATURES = 1024
 BLOCKS = FEATURES // P
-PIECE = 256
-GROUP = 4
+SPAN = 256
 
 FLOPS = 2 * ROLES * P * FEATURES * BALLS
 
@@ -23,40 +22,44 @@ def tile_temporaltransformer_kernel(tc, emb, pos, w, b, offs, out):
 
     bias_rows = b.rearrange("(p j) one -> p (j one)", j=BLOCKS)
     out_rows = out.rearrange("(p j) t -> p j t", j=BLOCKS)
+    pos_by_role = pos.rearrange("c (r t) -> c r t", r=ROLES)
 
-    with tc.tile_pool(name="held", bufs=1) as held, tc.psum_pool(name="psum", bufs=1) as psum:
+    with (
+        tc.tile_pool(name="held", bufs=1) as held,
+        tc.tile_pool(name="staged", bufs=BLOCKS) as staged,
+        tc.psum_pool(name="psum", bufs=BLOCKS) as psum,
+    ):
+        table = held.tile([P, PLAYERS], F32, name="table")
+        nc.sync.dma_start(table[:], emb)
         offsets = held.tile([P, ROLES * BALLS // 16], U16, name="offsets")
         nc.sync.dma_start(offsets[:], offs)
         bias = held.tile([P, BLOCKS], F32, name="bias")
         nc.sync.dma_start(bias[:], bias_rows)
-        table = held.tile([P, PLAYERS], F32, name="table")
-        nc.sync.dma_start(table[:], emb)
-        code = [held.tile([P, BALLS], F32, name=f"code{r}") for r in range(ROLES)]
-        for r in range(ROLES):
-            nc.sync.dma_start(code[r][:], pos[:, r * BALLS : (r + 1) * BALLS])
+        code = held.tile([P, ROLES, BALLS], F32, name="code")
+        for t0 in range(0, BALLS, SPAN):
+            nc.sync.dma_start(code[:, :, t0 : t0 + SPAN], pos_by_role[:, :, t0 : t0 + SPAN])
         weights = [held.tile([P, FEATURES], BF16, name=f"weights{r}") for r in range(ROLES)]
         for r in range(ROLES):
             nc.sync.dma_start(weights[r][:], w[r * P : (r + 1) * P, :])
-
-        summed = [held.tile([P, BALLS], F32, name=f"summed{r}") for r in range(ROLES)]
-        rounded = [held.tile([P, BALLS], BF16, name=f"rounded{r}") for r in range(ROLES)]
-        for r in range(ROLES):
-            for t0 in range(0, BALLS, PIECE):
-                first = (r * BALLS + t0) // 16
-                picked = table[:].indirect(offsets[:, first : first + PIECE // 16])
-                nc.vector.tensor_tensor(summed[r][:, t0 : t0 + PIECE], picked, code[r][:, t0 : t0 + PIECE], ADD)
-                nc.scalar.copy(rounded[r][:, t0 : t0 + PIECE], summed[r][:, t0 : t0 + PIECE])
-
         by_block = [weights[r][:].rearrange("c (p j) -> c j p", j=BLOCKS) for r in range(ROLES)]
-        banks = [psum.tile([P, BALLS], F32, name=f"bank{j}") for j in range(BLOCKS)]
-        result = held.tile([P, BLOCKS, BALLS], F32, name="result")
-        for j0 in range(0, BLOCKS, GROUP):
-            for j in range(j0, j0 + GROUP):
-                nc.tensor.matmul(banks[j][:], by_block[0][:, j, :], rounded[0][:], start=True, stop=False)
-            for j in range(j0, j0 + GROUP):
-                nc.tensor.matmul(banks[j][:], by_block[1][:, j, :], rounded[1][:], start=False, stop=True)
+
+        for t0 in range(0, BALLS, SPAN):
+            rounded = []
+            for r in range(ROLES):
+                first = (r * BALLS + t0) // 16
+                picked = table[:].indirect(offsets[:, first : first + SPAN // 16])
+                summed = held.tile([P, SPAN], F32, name=f"summed{r}_{t0}")
+                nc.vector.tensor_tensor(summed[:], picked, code[:, r, t0 : t0 + SPAN], ADD)
+                rounded.append(held.tile([P, SPAN], BF16, name=f"rounded{r}_{t0}"))
+                nc.scalar.copy(rounded[r][:], summed[:])
+
+            for j in range(BLOCKS):
+                acc = psum.tile([P, SPAN], F32, name="acc")
+                for r in range(ROLES):
+                    nc.tensor.matmul(acc[:], by_block[r][:, j, :], rounded[r][:], start=(r == 0), stop=(r == ROLES - 1))
+                result = staged.tile([P, SPAN], F32, name="result")
                 if j % 2 == 0:
-                    nc.scalar.activation(result[:, j, :], banks[j][:], IDENTITY, bias=bias[:, j : j + 1])
+                    nc.scalar.activation(result[:], acc[:], IDENTITY, bias=bias[:, j : j + 1])
                 else:
-                    nc.vector.tensor_scalar_add(result[:, j, :], banks[j][:], bias[:, j : j + 1])
-                nc.sync.dma_start(out_rows[:, j, :], result[:, j, :])
+                    nc.vector.tensor_scalar_add(result[:], acc[:], bias[:, j : j + 1])
+                nc.sync.dma_start(out_rows[:, j, t0 : t0 + SPAN], result[:])

@@ -13,6 +13,7 @@ ROLES = 2
 FEATURES = 1024
 BLOCKS = FEATURES // P
 SPAN = 256
+PAIR = 2
 
 FLOPS = 2 * ROLES * P * FEATURES * BALLS
 
@@ -24,11 +25,7 @@ def tile_temporaltransformer_kernel(tc, emb, pos, w, b, offs, out):
     out_rows = out.rearrange("(p j) t -> p j t", j=BLOCKS)
     pos_by_role = pos.rearrange("c (r t) -> c r t", r=ROLES)
 
-    with (
-        tc.tile_pool(name="held", bufs=1) as held,
-        tc.tile_pool(name="staged", bufs=BLOCKS) as staged,
-        tc.psum_pool(name="psum", bufs=BLOCKS) as psum,
-    ):
+    with tc.tile_pool(name="held", bufs=1) as held, tc.psum_pool(name="psum", bufs=BLOCKS) as psum:
         table = held.tile([P, PLAYERS], F32, name="table")
         nc.sync.dma_start(table[:], emb)
         offsets = held.tile([P, ROLES * BALLS // 16], U16, name="offsets")
@@ -53,13 +50,16 @@ def tile_temporaltransformer_kernel(tc, emb, pos, w, b, offs, out):
                 rounded.append(held.tile([P, SPAN], BF16, name=f"rounded{r}_{t0}"))
                 nc.scalar.copy(rounded[r][:], summed[:])
 
-            for j in range(BLOCKS):
-                acc = psum.tile([P, SPAN], F32, name="acc")
-                for r in range(ROLES):
-                    nc.tensor.matmul(acc[:], by_block[r][:, j, :], rounded[r][:], start=(r == 0), stop=(r == ROLES - 1))
-                result = staged.tile([P, SPAN], F32, name="result")
-                if j % 2 == 0:
-                    nc.scalar.activation(result[:], acc[:], IDENTITY, bias=bias[:, j : j + 1])
-                else:
-                    nc.vector.tensor_scalar_add(result[:], acc[:], bias[:, j : j + 1])
-                nc.sync.dma_start(out_rows[:, j, t0 : t0 + SPAN], result[:])
+            for j0 in range(0, BLOCKS, PAIR):
+                result = held.tile([P, PAIR, SPAN], F32, name=f"result{j0}_{t0}")
+                for j in range(j0, j0 + PAIR):
+                    acc = psum.tile([P, SPAN], F32, name="acc")
+                    for r in range(ROLES):
+                        nc.tensor.matmul(
+                            acc[:], by_block[r][:, j, :], rounded[r][:], start=(r == 0), stop=(r == ROLES - 1)
+                        )
+                    if j == j0:
+                        nc.scalar.activation(result[:, 0, :], acc[:], IDENTITY, bias=bias[:, j : j + 1])
+                    else:
+                        nc.vector.tensor_scalar_add(result[:, 1, :], acc[:], bias[:, j : j + 1])
+                nc.sync.dma_start(out_rows[:, j0 : j0 + PAIR, t0 : t0 + SPAN], result[:])

@@ -13,6 +13,7 @@ ROLES = 2
 FEATURES = 1024
 BLOCKS = FEATURES // P
 SPAN = 256
+WARM_UP = 13
 PAIR = 2
 
 FLOPS = 2 * ROLES * P * FEATURES * BALLS
@@ -39,6 +40,12 @@ def tile_temporaltransformer_kernel(tc, emb, pos, w, b, offs, out):
         for r in range(ROLES):
             nc.sync.dma_start(weights[r][:], w[r * P : (r + 1) * P, :])
         by_block = [weights[r][:].rearrange("c (p j) -> c j p", j=BLOCKS) for r in range(ROLES)]
+
+        zeros = held.tile([P, BALLS], BF16, name="zeros")
+        nc.vector.memset(zeros[:], 0.0)
+        idle = psum.tile([P, BALLS], F32, name="acc")
+        for i in range(WARM_UP):
+            nc.tensor.matmul(idle[:], zeros[:, 0:P], zeros[:], start=True, stop=True)
 
         for t0 in range(0, BALLS, SPAN):
             rounded = []

@@ -13,8 +13,10 @@ ROLES = 2
 FEATURES = 1024
 BLOCKS = FEATURES // P
 SPAN = 256
-WARM_UP = 13
+SPANS = BALLS // SPAN
+GROUP = 4
 PAIR = 2
+WARM_UP = 10
 
 FLOPS = 2 * ROLES * P * FEATURES * BALLS
 
@@ -24,21 +26,30 @@ def tile_temporaltransformer_kernel(tc, emb, pos, w, b, offs, out):
 
     bias_rows = b.rearrange("(p j) one -> p (j one)", j=BLOCKS)
     out_rows = out.rearrange("(p j) t -> p j t", j=BLOCKS)
-    pos_by_role = pos.rearrange("c (r t) -> c r t", r=ROLES)
 
     with tc.tile_pool(name="held", bufs=1) as held, tc.psum_pool(name="psum", bufs=BLOCKS) as psum:
-        table = held.tile([P, PLAYERS], F32, name="table")
-        nc.sync.dma_start(table[:], emb)
         offsets = held.tile([P, ROLES * BALLS // 16], U16, name="offsets")
-        nc.sync.dma_start(offsets[:], offs)
+        table = held.tile([P, PLAYERS], F32, name="table")
         bias = held.tile([P, BLOCKS], F32, name="bias")
-        nc.sync.dma_start(bias[:], bias_rows)
-        code = held.tile([P, ROLES, BALLS], F32, name="code")
-        for t0 in range(0, BALLS, SPAN):
-            nc.sync.dma_start(code[:, :, t0 : t0 + SPAN], pos_by_role[:, :, t0 : t0 + SPAN])
+        code = [[held.tile([P, SPAN], F32, name=f"code{r}_{s}") for s in range(SPANS)] for r in range(ROLES)]
         weights = [held.tile([P, FEATURES], BF16, name=f"weights{r}") for r in range(ROLES)]
-        for r in range(ROLES):
+
+        def load_code(r, s):
+            first = r * BALLS + s * SPAN
+            nc.sync.dma_start(code[r][s][:], pos[:, first : first + SPAN])
+
+        def load_weights(r):
             nc.sync.dma_start(weights[r][:], w[r * P : (r + 1) * P, :])
+
+        nc.sync.dma_start(offsets[:], offs)
+        nc.sync.dma_start(table[:], emb)
+        load_code(0, 0)
+        load_code(1, 0)
+        load_weights(0)
+        load_code(0, 1)
+        load_weights(1)
+        nc.sync.dma_start(bias[:], bias_rows)
+        load_code(1, 1)
         by_block = [weights[r][:].rearrange("c (p j) -> c j p", j=BLOCKS) for r in range(ROLES)]
 
         zeros = held.tile([P, BALLS], BF16, name="zeros")
@@ -47,26 +58,33 @@ def tile_temporaltransformer_kernel(tc, emb, pos, w, b, offs, out):
         for i in range(WARM_UP):
             nc.tensor.matmul(idle[:], zeros[:, 0:P], zeros[:], start=True, stop=True)
 
-        for t0 in range(0, BALLS, SPAN):
-            rounded = []
-            for r in range(ROLES):
-                first = (r * BALLS + t0) // 16
-                picked = table[:].indirect(offsets[:, first : first + SPAN // 16])
-                summed = held.tile([P, SPAN], F32, name=f"summed{r}_{t0}")
-                nc.vector.tensor_tensor(summed[:], picked, code[:, r, t0 : t0 + SPAN], ADD)
-                rounded.append(held.tile([P, SPAN], BF16, name=f"rounded{r}_{t0}"))
-                nc.scalar.copy(rounded[r][:], summed[:])
+        rounded = [[held.tile([P, SPAN], BF16, name=f"rounded{r}_{s}") for s in range(SPANS)] for r in range(ROLES)]
 
-            for j0 in range(0, BLOCKS, PAIR):
-                result = held.tile([P, PAIR, SPAN], F32, name=f"result{j0}_{t0}")
-                for j in range(j0, j0 + PAIR):
-                    acc = psum.tile([P, SPAN], F32, name="acc")
-                    for r in range(ROLES):
-                        nc.tensor.matmul(
-                            acc[:], by_block[r][:, j, :], rounded[r][:], start=(r == 0), stop=(r == ROLES - 1)
-                        )
-                    if j == j0:
-                        nc.scalar.activation(result[:, 0, :], acc[:], IDENTITY, bias=bias[:, j : j + 1])
-                    else:
-                        nc.vector.tensor_scalar_add(result[:, 1, :], acc[:], bias[:, j : j + 1])
-                nc.sync.dma_start(out_rows[:, j0 : j0 + PAIR, t0 : t0 + SPAN], result[:])
+        def look_up(s):
+            for r in range(ROLES):
+                first = (r * BALLS + s * SPAN) // 16
+                picked = table[:].indirect(offsets[:, first : first + SPAN // 16])
+                summed = held.tile([P, SPAN], F32, name=f"summed{r}_{s}")
+                nc.vector.tensor_tensor(summed[:], picked, code[r][s][:], ADD)
+                nc.scalar.copy(rounded[r][s][:], summed[:])
+
+        def project(s, j0):
+            group = range(j0, j0 + GROUP)
+            acc = {j: psum.tile([P, SPAN], F32, name="acc") for j in group}
+            for r in range(ROLES):
+                for j in group:
+                    nc.tensor.matmul(
+                        acc[j][:], by_block[r][:, j, :], rounded[r][s][:], start=(r == 0), stop=(r == ROLES - 1)
+                    )
+            for j1 in range(j0, j0 + GROUP, PAIR):
+                result = held.tile([P, PAIR, SPAN], F32, name=f"result{j1}_{s}")
+                nc.scalar.activation(result[:, 0, :], acc[j1][:], IDENTITY, bias=bias[:, j1 : j1 + 1])
+                nc.vector.tensor_scalar_add(result[:, 1, :], acc[j1 + 1][:], bias[:, j1 + 1 : j1 + 2])
+                nc.sync.dma_start(out_rows[:, j1 : j1 + PAIR, s * SPAN : (s + 1) * SPAN], result[:])
+
+        look_up(0)
+        for s in range(SPANS):
+            for j0 in range(0, BLOCKS, GROUP):
+                project(s, j0)
+                if j0 == 0 and s + 1 < SPANS:
+                    look_up(s + 1)

@@ -12,11 +12,12 @@ BALLS = 512
 ROLES = 2
 FEATURES = 1024
 BLOCKS = FEATURES // P
-SPAN = 256
-SPANS = BALLS // SPAN
+WIDTHS = (128, 128, 256)
+STARTS = (0, 128, 256)
+SPANS = len(WIDTHS)
 GROUP = 4
 PAIR = 2
-WARM_UP = 10
+WARM_UP = 9
 
 FLOPS = 2 * ROLES * P * FEATURES * BALLS
 
@@ -31,25 +32,22 @@ def tile_temporaltransformer_kernel(tc, emb, pos, w, b, offs, out):
         offsets = held.tile([P, ROLES * BALLS // 16], U16, name="offsets")
         table = held.tile([P, PLAYERS], F32, name="table")
         bias = held.tile([P, BLOCKS], F32, name="bias")
-        code = [[held.tile([P, SPAN], F32, name=f"code{r}_{s}") for s in range(SPANS)] for r in range(ROLES)]
+        code = [[held.tile([P, WIDTHS[s]], F32, name=f"code{r}_{s}") for s in range(SPANS)] for r in range(ROLES)]
         weights = [held.tile([P, FEATURES], BF16, name=f"weights{r}") for r in range(ROLES)]
 
-        def load_code(r, s):
-            first = r * BALLS + s * SPAN
-            nc.sync.dma_start(code[r][s][:], pos[:, first : first + SPAN])
-
-        def load_weights(r):
-            nc.sync.dma_start(weights[r][:], w[r * P : (r + 1) * P, :])
+        def load_code(s):
+            for r in range(ROLES):
+                first = r * BALLS + STARTS[s]
+                nc.sync.dma_start(code[r][s][:], pos[:, first : first + WIDTHS[s]])
 
         nc.sync.dma_start(offsets[:], offs)
         nc.sync.dma_start(table[:], emb)
-        load_code(0, 0)
-        load_code(1, 0)
-        load_weights(0)
-        load_code(0, 1)
-        load_weights(1)
+        load_code(0)
+        load_code(1)
+        for r in range(ROLES):
+            nc.sync.dma_start(weights[r][:], w[r * P : (r + 1) * P, :])
         nc.sync.dma_start(bias[:], bias_rows)
-        load_code(1, 1)
+        load_code(2)
         by_block = [weights[r][:].rearrange("c (p j) -> c j p", j=BLOCKS) for r in range(ROLES)]
 
         zeros = held.tile([P, BALLS], BF16, name="zeros")
@@ -58,33 +56,26 @@ def tile_temporaltransformer_kernel(tc, emb, pos, w, b, offs, out):
         for i in range(WARM_UP):
             nc.tensor.matmul(idle[:], zeros[:, 0:P], zeros[:], start=True, stop=True)
 
-        rounded = [[held.tile([P, SPAN], BF16, name=f"rounded{r}_{s}") for s in range(SPANS)] for r in range(ROLES)]
-
-        def look_up(s):
+        rounded = [[held.tile([P, WIDTHS[s]], BF16, name=f"rounded{r}_{s}") for s in range(SPANS)] for r in range(ROLES)]
+        for s in range(SPANS):
             for r in range(ROLES):
-                first = (r * BALLS + s * SPAN) // 16
-                picked = table[:].indirect(offsets[:, first : first + SPAN // 16])
-                summed = held.tile([P, SPAN], F32, name=f"summed{r}_{s}")
+                first = (r * BALLS + STARTS[s]) // 16
+                picked = table[:].indirect(offsets[:, first : first + WIDTHS[s] // 16])
+                summed = held.tile([P, WIDTHS[s]], F32, name=f"summed{r}_{s}")
                 nc.vector.tensor_tensor(summed[:], picked, code[r][s][:], ADD)
                 nc.scalar.copy(rounded[r][s][:], summed[:])
 
-        def project(s, j0):
-            group = range(j0, j0 + GROUP)
-            acc = {j: psum.tile([P, SPAN], F32, name="acc") for j in group}
-            for r in range(ROLES):
-                for j in group:
-                    nc.tensor.matmul(
-                        acc[j][:], by_block[r][:, j, :], rounded[r][s][:], start=(r == 0), stop=(r == ROLES - 1)
-                    )
-            for j1 in range(j0, j0 + GROUP, PAIR):
-                result = held.tile([P, PAIR, SPAN], F32, name=f"result{j1}_{s}")
-                nc.scalar.activation(result[:, 0, :], acc[j1][:], IDENTITY, bias=bias[:, j1 : j1 + 1])
-                nc.vector.tensor_scalar_add(result[:, 1, :], acc[j1 + 1][:], bias[:, j1 + 1 : j1 + 2])
-                nc.sync.dma_start(out_rows[:, j1 : j1 + PAIR, s * SPAN : (s + 1) * SPAN], result[:])
-
-        look_up(0)
         for s in range(SPANS):
             for j0 in range(0, BLOCKS, GROUP):
-                project(s, j0)
-                if j0 == 0 and s + 1 < SPANS:
-                    look_up(s + 1)
+                group = range(j0, j0 + GROUP)
+                acc = {j: psum.tile([P, WIDTHS[s]], F32, name="acc") for j in group}
+                for r in range(ROLES):
+                    for j in group:
+                        nc.tensor.matmul(
+                            acc[j][:], by_block[r][:, j, :], rounded[r][s][:], start=(r == 0), stop=(r == ROLES - 1)
+                        )
+                for j1 in range(j0, j0 + GROUP, PAIR):
+                    result = held.tile([P, PAIR, WIDTHS[s]], F32, name=f"result{j1}_{s}")
+                    nc.scalar.activation(result[:, 0, :], acc[j1][:], IDENTITY, bias=bias[:, j1 : j1 + 1])
+                    nc.vector.tensor_scalar_add(result[:, 1, :], acc[j1 + 1][:], bias[:, j1 + 1 : j1 + 2])
+                    nc.sync.dma_start(out_rows[:, j1 : j1 + PAIR, STARTS[s] : STARTS[s] + WIDTHS[s]], result[:])

import concourse.mybir as mybir

F32 = mybir.dt.float32
BF16 = mybir.dt.bfloat16
U16 = mybir.dt.uint16
ADD = mybir.AluOpType.add
IDENTITY = mybir.ActivationFunctionType.Identity

P = 128
PLAYERS = 2048
BALLS = 512
ROLES = 2
FEATURES = 1024
BLOCKS = FEATURES // P
WIDTHS = (128, 128, 256)
STARTS = (0, 128, 256)
SPANS = len(WIDTHS)
GROUP = 4
PAIR = 2
WARM_UP = 9

FLOPS = 2 * ROLES * P * FEATURES * BALLS


def tile_temporaltransformer_kernel(tc, emb, pos, w, b, offs, out):
    nc = tc.nc

    bias_rows = b.rearrange("(p j) one -> p (j one)", j=BLOCKS)
    out_rows = out.rearrange("(p j) t -> p j t", j=BLOCKS)

    with tc.tile_pool(name="held", bufs=1) as held, tc.psum_pool(name="psum", bufs=BLOCKS) as psum:
        offsets = held.tile([P, ROLES * BALLS // 16], U16, name="offsets")
        table = held.tile([P, PLAYERS], F32, name="table")
        bias = held.tile([P, BLOCKS], F32, name="bias")
        code = [[held.tile([P, WIDTHS[s]], F32, name=f"code{r}_{s}") for s in range(SPANS)] for r in range(ROLES)]
        weights = [held.tile([P, FEATURES], BF16, name=f"weights{r}") for r in range(ROLES)]

        def load_code(s):
            for r in range(ROLES):
                first = r * BALLS + STARTS[s]
                nc.sync.dma_start(code[r][s][:], pos[:, first : first + WIDTHS[s]])

        nc.sync.dma_start(offsets[:], offs)
        nc.sync.dma_start(table[:], emb)
        load_code(0)
        load_code(1)
        for r in range(ROLES):
            nc.sync.dma_start(weights[r][:], w[r * P : (r + 1) * P, :])
        nc.sync.dma_start(bias[:], bias_rows)
        load_code(2)
        by_block = [weights[r][:].rearrange("c (p j) -> c j p", j=BLOCKS) for r in range(ROLES)]

        zeros = held.tile([P, BALLS], BF16, name="zeros")
        nc.vector.memset(zeros[:], 0.0)
        idle = psum.tile([P, BALLS], F32, name="acc")
        for i in range(WARM_UP):
            nc.tensor.matmul(idle[:], zeros[:, 0:P], zeros[:], start=True, stop=True)

        rounded = [[held.tile([P, WIDTHS[s]], BF16, name=f"rounded{r}_{s}") for s in range(SPANS)] for r in range(ROLES)]
        for s in range(SPANS):
            for r in range(ROLES):
                first = (r * BALLS + STARTS[s]) // 16
                picked = table[:].indirect(offsets[:, first : first + WIDTHS[s] // 16])
                summed = held.tile([P, WIDTHS[s]], F32, name=f"summed{r}_{s}")
                nc.vector.tensor_tensor(summed[:], picked, code[r][s][:], ADD)
                nc.scalar.copy(rounded[r][s][:], summed[:])

        for s in range(SPANS):
            for j0 in range(0, BLOCKS, GROUP):
                group = range(j0, j0 + GROUP)
                acc = {j: psum.tile([P, WIDTHS[s]], F32, name="acc") for j in group}
                for r in range(ROLES):
                    for j in group:
                        nc.tensor.matmul(
                            acc[j][:], by_block[r][:, j, :], rounded[r][s][:], start=(r == 0), stop=(r == ROLES - 1)
                        )
                for j1 in range(j0, j0 + GROUP, PAIR):
                    result = held.tile([P, PAIR, WIDTHS[s]], F32, name=f"result{j1}_{s}")
                    nc.scalar.activation(result[:, 0, :], acc[j1][:], IDENTITY, bias=bias[:, j1 : j1 + 1])
                    nc.vector.tensor_scalar_add(result[:, 1, :], acc[j1 + 1][:], bias[:, j1 + 1 : j1 + 2])
                    nc.sync.dma_start(out_rows[:, j1 : j1 + PAIR, STARTS[s] : STARTS[s] + WIDTHS[s]], result[:])
